import numpy as np
import ml_dtypes


def mxq(x, axis, fmt="e4m3"):
    dtype, down = {"e4m3": (ml_dtypes.float8_e4m3fn, 7), "e5m2": (ml_dtypes.float8_e5m2, 14)}[fmt]
    v = np.moveaxis(np.asarray(x, np.float32).astype(ml_dtypes.bfloat16).astype(np.float64), axis, -1)
    blocks = v.reshape(v.shape[:-1] + (-1, 32))
    amax = np.abs(blocks).max(-1, keepdims=True)
    byte = np.maximum(np.where(amax > 0, np.frexp(amax)[1] - 1 + 127, 0) - down, 1)
    scale = np.exp2(byte - 127.0)
    codes = (blocks / scale).astype(np.float32).astype(dtype).astype(np.float64)
    return np.moveaxis((codes * scale).reshape(v.shape), -1, axis)


WIDE = False


def mx_kscale(k):
    if not WIDE:
        return np.ones(k)
    levels = np.array([20, -20, 10, -10, 0])
    a = np.random.permutation(np.resize(levels, k // 512 * 4)).reshape(k // 512, 4)
    idx = np.arange(k)
    return np.exp2(a[idx // 512, idx % 128 // 32])


BF16 = ml_dtypes.bfloat16


def bf(x):
    return np.asarray(x, np.float32).astype(BF16)


def f64(x):
    return np.asarray(x).astype(np.float64)


BS, P, C, D, E = 512, 1152, 32, 16, 8
K = P * E
N = C * D
G_SCALE = float(P)


def routed_sum(x, W):
    xf = f64(x).reshape(BS, K)
    wf = f64(W)[0].transpose(0, 3, 1, 2).reshape(K, N)
    return (xf @ wf / P).reshape(BS, C, D)


def setup_inputs():
    ks = mx_kscale(BS)
    x0 = bf(np.random.standard_normal((BS, P, E)))
    W = bf(np.random.standard_normal((1, P, C, D, E)) * np.sqrt(P / E))
    g = bf(np.random.standard_normal((BS, C, D, 1)) * np.exp2(np.random.randint(-12, 1, (BS, 1, 1, 1))) * G_SCALE / ks[:, None, None, None])
    s = routed_sum(x0, W)
    return {"x": bf(f64(x0) * ks[:, None, None]), "W": W, "s": np.asarray(s, np.float32), "grad_out": g}


def reference(x, W, s, grad_out):
    sf = f64(s).reshape(BS, N)
    ds = f64(grad_out).reshape(BS, N) * (2.0 * np.abs(sf) / (1.0 + sf * sf) ** 2)
    xf = f64(x).reshape(BS, K)
    gw = (mxq(xf, 0, "e4m3").T @ mxq(ds, 0, "e5m2")) / P
    return gw.reshape(P, E, C, D).transpose(0, 2, 3, 1)[None]

@@ -1,0 +1,127 @@
+import concourse.mybir as mybir
+
+F32 = mybir.dt.float32
+BF16 = mybir.dt.bfloat16
+U32 = mybir.dt.uint32
+U8 = mybir.dt.uint8
+E4M3_X4 = mybir.dt.float8_e4m3fn_x4
+E5M2_X4 = mybir.dt.float8_e5m2_x4
+ACT = mybir.ActivationFunctionType
+
+PARTS = 128
+PACK = 4
+BATCH = PARTS * PACK
+CAPS = 1152
+E = 8
+N = 512
+Q_TILE = PARTS
+TILES = CAPS // Q_TILE
+TILE_COLS = Q_TILE * E
+E_HALF = E // 2
+N_CHUNK = 128
+HEAD_TILES = 4
+
+FLOPS = 2 * BATCH * CAPS * E * N
+BYTES = BATCH * CAPS * E * 2 + BATCH * N * 4 + BATCH * N * 2 + CAPS * E * N * 4
+
+
+def tile_digitcaps_v_kernel(tc, x, W, s, grad_out, out):
+    nc = tc.nc
+
+    x_rows = x.rearrange("(p j) q e -> p j (q e)", j=PACK)
+    s_rows = s.rearrange("(p j) c d -> p j (c d)", j=PACK)
+    g_rows = grad_out.rearrange("(p j) c d o -> p j (c d o)", j=PACK)
+    out_rows = out.rearrange("o q c d e -> (o q) (c d e)")
+
+    with tc.tile_pool(name="keep", bufs=1) as keep, tc.tile_pool(name="work", bufs=3) as work:
+        ds_codes = keep.tile([PARTS, N], U32, align_bytes=64)
+        ds_scales = keep.tile([PARTS, N], U8, align_bytes=64)
+        x_sb = []
+
+        with tc.tile_pool(name="head", bufs=1) as head:
+            s_sb = head.tile([PARTS, PACK, N], F32)
+            nc.sync.dma_start(out=s_sb[:], in_=s_rows)
+            g_sb = head.tile([PARTS, PACK, N], BF16)
+            nc.sync.dma_start(out=g_sb[:], in_=g_rows)
+            for t in range(TILES):
+                x_tile = keep.tile([PARTS, PACK, TILE_COLS], BF16, name="x_tile%d" % t)
+                nc.sync.dma_start(
+                    out=x_tile[:], in_=x_rows[:, :, t * TILE_COLS : (t + 1) * TILE_COLS]
+                )
+                x_sb.append(x_tile)
+
+            twice_abs = head.tile([PARTS, N, PACK], F32)
+            denom = head.tile([PARTS, N, PACK], F32)
+            ds_bf = head.tile([PARTS, N, PACK], BF16, align_bytes=64)
+            for chunk in range(N // N_CHUNK):
+                n_cols = slice(chunk * N_CHUNK, (chunk + 1) * N_CHUNK)
+                s_nj = s_sb[:, :, n_cols].rearrange("p j n -> p n j")
+                g_nj = g_sb[:, :, n_cols].rearrange("p j n -> p n j")
+                nc.scalar.activation(out=denom[:, n_cols, :], in_=s_nj, func=ACT.Square)
+                nc.scalar.activation(
+                    out=denom[:, n_cols, :], in_=denom[:, n_cols, :], func=ACT.Square, bias=1.0
+                )
+                nc.scalar.activation(
+                    out=twice_abs[:, n_cols, :], in_=s_nj, func=ACT.Abs, scale=2.0
+                )
+                nc.vector.reciprocal(out=denom[:, n_cols, :], in_=denom[:, n_cols, :])
+                nc.vector.tensor_mul(
+                    out=twice_abs[:, n_cols, :], in0=twice_abs[:, n_cols, :], in1=g_nj
+                )
+                nc.vector.tensor_mul(
+                    out=ds_bf[:, n_cols, :], in0=twice_abs[:, n_cols, :], in1=denom[:, n_cols, :]
+                )
+            nc.vector.quantize_mx(
+                out=ds_codes[:].bitcast(E5M2_X4),
+                scales=ds_scales[:],
+                in_=ds_bf[:].rearrange("p n j -> p (n j)"),
+            )
+
+        with (
+            tc.tile_pool(name="flats", bufs=2) as flats,
+            tc.tile_pool(name="stores", bufs=3) as stores,
+            tc.psum_pool(name="psum", bufs=8) as psum,
+        ):
+            for t in range(TILES):
+                x_qje = x_sb[t][:].rearrange("p j (q e) -> p q j e", e=E)
+                grouped = work.tile([PARTS, E, Q_TILE, PACK], BF16, align_bytes=64)
+                regroup = nc.scalar.copy if t < HEAD_TILES else nc.vector.tensor_copy
+                for half in range(2):
+                    es = slice(half * E_HALF, (half + 1) * E_HALF)
+                    regroup(
+                        out=grouped[:, es, :, :].rearrange("p e q j -> p q j e"),
+                        in_=x_qje[:, :, :, es],
+                    )
+                x_codes = keep.tile([PARTS, TILE_COLS], U32, align_bytes=64, name="x_codes%d" % t)
+                x_scales = keep.tile([PARTS, TILE_COLS], U8, align_bytes=64, name="x_scales%d" % t)
+                nc.vector.quantize_mx(
+                    out=x_codes[:].bitcast(E4M3_X4),
+                    scales=x_scales[:],
+                    in_=grouped[:].rearrange("p e q j -> p (e q j)"),
+                )
+
+                flat = flats.tile([PARTS, E, N], F32)
+                for e in range(E):
+                    q_cols = slice(e * Q_TILE, (e + 1) * Q_TILE)
+                    acc = psum.tile([PARTS, N], F32)
+                    nc.tensor.matmul_mx(
+                        out=acc[:],
+                        lhsT=x_codes[:, q_cols].bitcast(E4M3_X4),
+                        lhsT_scale=x_scales[:, q_cols],
+                        rhs=ds_codes[:].bitcast(E5M2_X4),
+                        rhs_scale=ds_scales[:],
+                        start=True,
+                        stop=True,
+                    )
+                    nc.scalar.mul(out=flat[:, e, :], in_=acc[:], mul=1.0 / CAPS)
+
+                stage = stores.tile([PARTS, N, E], F32)
+                for half in range(2):
+                    es = slice(half * E_HALF, (half + 1) * E_HALF)
+                    nc.vector.tensor_copy(
+                        out=stage[:, :, es], in_=flat[:, es, :].rearrange("p e n -> p n e")
+                    )
+                nc.sync.dma_start(
+                    out=out_rows[t * Q_TILE : (t + 1) * Q_TILE, :],
+                    in_=stage[:].rearrange("p n e -> p (n e)"),
+                )

@@ -19,10 +19,13 @@ TILES = CAPS // Q_TILE
 TILE_COLS = Q_TILE * E
 E_HALF = E // 2
 N_CHUNK = 128
-HEAD_TILES = 4
+N_HALF = N // 2
+BIG = 3.0e38
+SCALAR_TILES = range(3, 5)
 
 FLOPS = 2 * BATCH * CAPS * E * N
 BYTES = BATCH * CAPS * E * 2 + BATCH * N * 4 + BATCH * N * 2 + CAPS * E * N * 4
+ALU = mybir.AluOpType
 
 
 def tile_digitcaps_v_kernel(tc, x, W, s, grad_out, out):
@@ -36,40 +39,69 @@ def tile_digitcaps_v_kernel(tc, x, W, s, grad_out, out):
     with tc.tile_pool(name="keep", bufs=1) as keep, tc.tile_pool(name="work", bufs=3) as work:
         ds_codes = keep.tile([PARTS, N], U32, align_bytes=64)
         ds_scales = keep.tile([PARTS, N], U8, align_bytes=64)
-        x_sb = []
+        x_sb = [
+            keep.tile([PARTS, PACK, TILE_COLS], BF16, name="x_tile%d" % t) for t in range(TILES)
+        ]
+
+        def load_x(t):
+            nc.sync.dma_start(
+                out=x_sb[t][:], in_=x_rows[:, :, t * TILE_COLS : (t + 1) * TILE_COLS]
+            )
 
         with tc.tile_pool(name="head", bufs=1) as head:
             s_sb = head.tile([PARTS, PACK, N], F32)
-            nc.sync.dma_start(out=s_sb[:], in_=s_rows)
             g_sb = head.tile([PARTS, PACK, N], BF16)
+            nc.sync.dma_start(out=s_sb[:], in_=s_rows)
+            load_x(0)
             nc.sync.dma_start(out=g_sb[:], in_=g_rows)
-            for t in range(TILES):
-                x_tile = keep.tile([PARTS, PACK, TILE_COLS], BF16, name="x_tile%d" % t)
-                nc.sync.dma_start(
-                    out=x_tile[:], in_=x_rows[:, :, t * TILE_COLS : (t + 1) * TILE_COLS]
-                )
-                x_sb.append(x_tile)
+            for t in range(1, TILES):
+                load_x(t)
 
-            twice_abs = head.tile([PARTS, N, PACK], F32)
+            s_nj = s_sb[:].rearrange("p j n -> p n j")
+            g_nj = g_sb[:].rearrange("p j n -> p n j")
+            weight = head.tile([PARTS, N, PACK], F32)
             denom = head.tile([PARTS, N, PACK], F32)
+            recip = head.tile([PARTS, N, PACK], F32)
+            check = head.tile([PARTS, N, PACK], F32)
             ds_bf = head.tile([PARTS, N, PACK], BF16, align_bytes=64)
-            for chunk in range(N // N_CHUNK):
-                n_cols = slice(chunk * N_CHUNK, (chunk + 1) * N_CHUNK)
-                s_nj = s_sb[:, :, n_cols].rearrange("p j n -> p n j")
-                g_nj = g_sb[:, :, n_cols].rearrange("p j n -> p n j")
-                nc.scalar.activation(out=denom[:, n_cols, :], in_=s_nj, func=ACT.Square)
+            chunks = [slice(c * N_CHUNK, (c + 1) * N_CHUNK) for c in range(N // N_CHUNK)]
+            nc.scalar.activation(out=weight[:], in_=s_nj, func=ACT.Abs, scale=2.0)
+            nc.vector.scalar_tensor_tensor(
+                out=weight[:], in0=weight[:], scalar=-1.0, in1=g_nj, op0=ALU.mult, op1=ALU.mult
+            )
+            for n_cols in chunks:
+                nc.scalar.activation(out=denom[:, n_cols, :], in_=s_nj[:, n_cols, :], func=ACT.Square)
+            for n_cols in chunks:
                 nc.scalar.activation(
                     out=denom[:, n_cols, :], in_=denom[:, n_cols, :], func=ACT.Square, bias=1.0
                 )
+            for n_cols in chunks:
                 nc.scalar.activation(
-                    out=twice_abs[:, n_cols, :], in_=s_nj, func=ACT.Abs, scale=2.0
+                    out=recip[:, n_cols, :], in_=denom[:, n_cols, :], func=ACT.Abs_reciprocal_sqrt
                 )
-                nc.vector.reciprocal(out=denom[:, n_cols, :], in_=denom[:, n_cols, :])
-                nc.vector.tensor_mul(
-                    out=twice_abs[:, n_cols, :], in0=twice_abs[:, n_cols, :], in1=g_nj
+            for n_cols in chunks:
+                nc.scalar.activation(out=recip[:, n_cols, :], in_=recip[:, n_cols, :], func=ACT.Square)
+            for n_cols in chunks:
+                nc.vector.scalar_tensor_tensor(
+                    out=check[:, n_cols, :],
+                    in0=denom[:, n_cols, :],
+                    scalar=BIG,
+                    in1=recip[:, n_cols, :],
+                    op0=ALU.min,
+                    op1=ALU.mult,
                 )
+            for n_cols in chunks:
+                nc.vector.scalar_tensor_tensor(
+                    out=check[:, n_cols, :],
+                    in0=check[:, n_cols, :],
+                    scalar=2.0,
+                    in1=recip[:, n_cols, :],
+                    op0=ALU.subtract,
+                    op1=ALU.mult,
+                )
+            for n_cols in chunks:
                 nc.vector.tensor_mul(
-                    out=ds_bf[:, n_cols, :], in0=twice_abs[:, n_cols, :], in1=denom[:, n_cols, :]
+                    out=ds_bf[:, n_cols, :], in0=weight[:, n_cols, :], in1=check[:, n_cols, :]
                 )
             nc.vector.quantize_mx(
                 out=ds_codes[:].bitcast(E5M2_X4),
@@ -79,13 +111,13 @@ def tile_digitcaps_v_kernel(tc, x, W, s, grad_out, out):
 
         with (
             tc.tile_pool(name="flats", bufs=2) as flats,
-            tc.tile_pool(name="stores", bufs=3) as stores,
+            tc.tile_pool(name="stores", bufs=6) as stores,
             tc.psum_pool(name="psum", bufs=8) as psum,
         ):
             for t in range(TILES):
                 x_qje = x_sb[t][:].rearrange("p j (q e) -> p q j e", e=E)
                 grouped = work.tile([PARTS, E, Q_TILE, PACK], BF16, align_bytes=64)
-                regroup = nc.scalar.copy if t < HEAD_TILES else nc.vector.tensor_copy
+                regroup = nc.scalar.copy if t in SCALAR_TILES else nc.vector.tensor_copy
                 for half in range(2):
                     es = slice(half * E_HALF, (half + 1) * E_HALF)
                     regroup(
@@ -115,13 +147,19 @@ def tile_digitcaps_v_kernel(tc, x, W, s, grad_out, out):
                     )
                     nc.scalar.mul(out=flat[:, e, :], in_=acc[:], mul=1.0 / CAPS)
 
-                stage = stores.tile([PARTS, N, E], F32)
-                for half in range(2):
-                    es = slice(half * E_HALF, (half + 1) * E_HALF)
-                    nc.vector.tensor_copy(
-                        out=stage[:, :, es], in_=flat[:, es, :].rearrange("p e n -> p n e")
+                stages = [stores.tile([PARTS, N_HALF, E], F32, name="stage") for h in range(2)]
+                for e_half in range(2):
+                    es = slice(e_half * E_HALF, (e_half + 1) * E_HALF)
+                    for n_half in range(2):
+                        ns = slice(n_half * N_HALF, (n_half + 1) * N_HALF)
+                        nc.vector.tensor_copy(
+                            out=stages[n_half][:, :, es],
+                            in_=flat[:, es, ns].rearrange("p e n -> p n e"),
+                        )
+                for n_half in range(2):
+                    nc.sync.dma_start(
+                        out=out_rows[
+                            t * Q_TILE : (t + 1) * Q_TILE, n_half * N_HALF * E : (n_half + 1) * N_HALF * E
+                        ],
+                        in_=stages[n_half][:].rearrange("p n e -> p (n e)"),
                     )
-                nc.sync.dma_start(
-                    out=out_rows[t * Q_TILE : (t + 1) * Q_TILE, :],
-                    in_=stage[:].rearrange("p n e -> p (n e)"),
-                )

@@ -21,7 +21,7 @@ E_HALF = E // 2
 N_CHUNK = 128
 N_HALF = N // 2
 BIG = 3.0e38
-SCALAR_TILES = range(3, 5)
+SCALAR_TILE = 1
 
 FLOPS = 2 * BATCH * CAPS * E * N
 BYTES = BATCH * CAPS * E * 2 + BATCH * N * 4 + BATCH * N * 2 + CAPS * E * N * 4
@@ -43,19 +43,21 @@ def tile_digitcaps_v_kernel(tc, x, W, s, grad_out, out):
             keep.tile([PARTS, PACK, TILE_COLS], BF16, name="x_tile%d" % t) for t in range(TILES)
         ]
 
-        def load_x(t):
-            nc.sync.dma_start(
-                out=x_sb[t][:], in_=x_rows[:, :, t * TILE_COLS : (t + 1) * TILE_COLS]
-            )
-
         with tc.tile_pool(name="head", bufs=1) as head:
+            warm = head.tile([PARTS, 2], F32)
+            nc.vector.memset(warm[:, 0:1], 1.0)
+            nc.scalar.activation(out=warm[:, 1:2], in_=warm[:, 0:1], func=ACT.Abs_reciprocal_sqrt)
+
             s_sb = head.tile([PARTS, PACK, N], F32)
             g_sb = head.tile([PARTS, PACK, N], BF16)
-            nc.sync.dma_start(out=s_sb[:], in_=s_rows)
-            load_x(0)
+            for n_half in range(2):
+                ns = slice(n_half * N_HALF, (n_half + 1) * N_HALF)
+                nc.sync.dma_start(out=s_sb[:, :, ns], in_=s_rows[:, :, ns])
             nc.sync.dma_start(out=g_sb[:], in_=g_rows)
-            for t in range(1, TILES):
-                load_x(t)
+            for t in range(TILES):
+                nc.sync.dma_start(
+                    out=x_sb[t][:], in_=x_rows[:, :, t * TILE_COLS : (t + 1) * TILE_COLS]
+                )
 
             s_nj = s_sb[:].rearrange("p j n -> p n j")
             g_nj = g_sb[:].rearrange("p j n -> p n j")
@@ -64,50 +66,73 @@ def tile_digitcaps_v_kernel(tc, x, W, s, grad_out, out):
             recip = head.tile([PARTS, N, PACK], F32)
             check = head.tile([PARTS, N, PACK], F32)
             ds_bf = head.tile([PARTS, N, PACK], BF16, align_bytes=64)
-            chunks = [slice(c * N_CHUNK, (c + 1) * N_CHUNK) for c in range(N // N_CHUNK)]
-            nc.scalar.activation(out=weight[:], in_=s_nj, func=ACT.Abs, scale=2.0)
-            nc.vector.scalar_tensor_tensor(
-                out=weight[:], in0=weight[:], scalar=-1.0, in1=g_nj, op0=ALU.mult, op1=ALU.mult
-            )
-            for n_cols in chunks:
-                nc.scalar.activation(out=denom[:, n_cols, :], in_=s_nj[:, n_cols, :], func=ACT.Square)
-            for n_cols in chunks:
-                nc.scalar.activation(
-                    out=denom[:, n_cols, :], in_=denom[:, n_cols, :], func=ACT.Square, bias=1.0
-                )
-            for n_cols in chunks:
-                nc.scalar.activation(
-                    out=recip[:, n_cols, :], in_=denom[:, n_cols, :], func=ACT.Abs_reciprocal_sqrt
-                )
-            for n_cols in chunks:
-                nc.scalar.activation(out=recip[:, n_cols, :], in_=recip[:, n_cols, :], func=ACT.Square)
-            for n_cols in chunks:
+            for n_half in range(2):
+                ns = slice(n_half * N_HALF, (n_half + 1) * N_HALF)
+                chunks = [
+                    slice(n_half * N_HALF + c * N_CHUNK, n_half * N_HALF + (c + 1) * N_CHUNK)
+                    for c in range(N_HALF // N_CHUNK)
+                ]
                 nc.vector.scalar_tensor_tensor(
-                    out=check[:, n_cols, :],
-                    in0=denom[:, n_cols, :],
-                    scalar=BIG,
-                    in1=recip[:, n_cols, :],
-                    op0=ALU.min,
+                    out=weight[:, ns, :],
+                    in0=s_nj[:, ns, :],
+                    scalar=-1.0,
+                    in1=s_nj[:, ns, :],
+                    op0=ALU.mult,
+                    op1=ALU.max,
+                )
+                nc.vector.scalar_tensor_tensor(
+                    out=weight[:, ns, :],
+                    in0=weight[:, ns, :],
+                    scalar=-2.0,
+                    in1=g_nj[:, ns, :],
+                    op0=ALU.mult,
                     op1=ALU.mult,
                 )
-            for n_cols in chunks:
-                nc.vector.scalar_tensor_tensor(
-                    out=check[:, n_cols, :],
-                    in0=check[:, n_cols, :],
-                    scalar=2.0,
-                    in1=recip[:, n_cols, :],
-                    op0=ALU.subtract,
-                    op1=ALU.mult,
+                for n_cols in chunks:
+                    nc.scalar.activation(
+                        out=denom[:, n_cols, :], in_=s_nj[:, n_cols, :], func=ACT.Square
+                    )
+                for n_cols in chunks:
+                    nc.scalar.activation(
+                        out=denom[:, n_cols, :], in_=denom[:, n_cols, :], func=ACT.Square, bias=1.0
+                    )
+                for n_cols in chunks:
+                    nc.scalar.activation(
+                        out=recip[:, n_cols, :],
+                        in_=denom[:, n_cols, :],
+                        func=ACT.Abs_reciprocal_sqrt,
+                    )
+                for n_cols in chunks:
+                    nc.scalar.activation(
+                        out=recip[:, n_cols, :], in_=recip[:, n_cols, :], func=ACT.Square
+                    )
+                for n_cols in chunks:
+                    nc.vector.scalar_tensor_tensor(
+                        out=check[:, n_cols, :],
+                        in0=denom[:, n_cols, :],
+                        scalar=BIG,
+                        in1=recip[:, n_cols, :],
+                        op0=ALU.min,
+                        op1=ALU.mult,
+                    )
+                for n_cols in chunks:
+                    nc.vector.scalar_tensor_tensor(
+                        out=check[:, n_cols, :],
+                        in0=check[:, n_cols, :],
+                        scalar=2.0,
+                        in1=recip[:, n_cols, :],
+                        op0=ALU.subtract,
+                        op1=ALU.mult,
+                    )
+                for n_cols in chunks:
+                    nc.vector.tensor_mul(
+                        out=ds_bf[:, n_cols, :], in0=weight[:, n_cols, :], in1=check[:, n_cols, :]
+                    )
+                nc.vector.quantize_mx(
+                    out=ds_codes[:, ns].bitcast(E5M2_X4),
+                    scales=ds_scales[:, ns],
+                    in_=ds_bf[:, ns, :].rearrange("p n j -> p (n j)"),
                 )
-            for n_cols in chunks:
-                nc.vector.tensor_mul(
-                    out=ds_bf[:, n_cols, :], in0=weight[:, n_cols, :], in1=check[:, n_cols, :]
-                )
-            nc.vector.quantize_mx(
-                out=ds_codes[:].bitcast(E5M2_X4),
-                scales=ds_scales[:],
-                in_=ds_bf[:].rearrange("p n j -> p (n j)"),
-            )
 
         with (
             tc.tile_pool(name="flats", bufs=2) as flats,
@@ -117,7 +142,7 @@ def tile_digitcaps_v_kernel(tc, x, W, s, grad_out, out):
             for t in range(TILES):
                 x_qje = x_sb[t][:].rearrange("p j (q e) -> p q j e", e=E)
                 grouped = work.tile([PARTS, E, Q_TILE, PACK], BF16, align_bytes=64)
-                regroup = nc.scalar.copy if t in SCALAR_TILES else nc.vector.tensor_copy
+                regroup = nc.scalar.copy if t == SCALAR_TILE else nc.vector.tensor_copy
                 for half in range(2):
                     es = slice(half * E_HALF, (half + 1) * E_HALF)
                     regroup(

@@ -21,7 +21,7 @@ E_HALF = E // 2
 N_CHUNK = 128
 N_HALF = N // 2
 BIG = 3.0e38
-SCALAR_TILE = 1
+SCALAR_TILES = (1, 2)
 
 FLOPS = 2 * BATCH * CAPS * E * N
 BYTES = BATCH * CAPS * E * 2 + BATCH * N * 4 + BATCH * N * 2 + CAPS * E * N * 4
@@ -142,7 +142,7 @@ def tile_digitcaps_v_kernel(tc, x, W, s, grad_out, out):
             for t in range(TILES):
                 x_qje = x_sb[t][:].rearrange("p j (q e) -> p q j e", e=E)
                 grouped = work.tile([PARTS, E, Q_TILE, PACK], BF16, align_bytes=64)
-                regroup = nc.scalar.copy if t == SCALAR_TILE else nc.vector.tensor_copy
+                regroup = nc.scalar.copy if t in SCALAR_TILES else nc.vector.tensor_copy
                 for half in range(2):
                     es = slice(half * E_HALF, (half + 1) * E_HALF)
                     regroup(

@@ -178,8 +178,8 @@ def tile_digitcaps_v_kernel(tc, x, W, s, grad_out, out):
                     for n_half in range(2):
                         ns = slice(n_half * N_HALF, (n_half + 1) * N_HALF)
                         nc.vector.tensor_copy(
-                            out=stages[n_half][:, :, es],
-                            in_=flat[:, es, ns].rearrange("p e n -> p n e"),
+                            out=stages[n_half][:, :, es].rearrange("p (m i) e -> p m e i", i=2),
+                            in_=flat[:, es, ns].rearrange("p e (m i) -> p m e i", i=2),
                         )
                 for n_half in range(2):
                     nc.sync.dma_start(

@@ -59,12 +59,10 @@ def tile_digitcaps_v_kernel(tc, x, W, s, grad_out, out):
                     out=x_sb[t][:], in_=x_rows[:, :, t * TILE_COLS : (t + 1) * TILE_COLS]
                 )
 
-            s_nj = s_sb[:].rearrange("p j n -> p n j")
-            g_nj = g_sb[:].rearrange("p j n -> p n j")
-            weight = head.tile([PARTS, N, PACK], F32)
-            denom = head.tile([PARTS, N, PACK], F32)
-            recip = head.tile([PARTS, N, PACK], F32)
-            check = head.tile([PARTS, N, PACK], F32)
+            weight = head.tile([PARTS, PACK, N], F32)
+            denom = head.tile([PARTS, PACK, N], F32)
+            recip = head.tile([PARTS, PACK, N], F32)
+            check = head.tile([PARTS, PACK, N], F32)
             ds_bf = head.tile([PARTS, N, PACK], BF16, align_bytes=64)
             for n_half in range(2):
                 ns = slice(n_half * N_HALF, (n_half + 1) * N_HALF)
@@ -73,60 +71,63 @@ def tile_digitcaps_v_kernel(tc, x, W, s, grad_out, out):
                     for c in range(N_HALF // N_CHUNK)
                 ]
                 nc.vector.scalar_tensor_tensor(
-                    out=weight[:, ns, :],
-                    in0=s_nj[:, ns, :],
+                    out=weight[:, :, ns],
+                    in0=s_sb[:, :, ns],
                     scalar=-1.0,
-                    in1=s_nj[:, ns, :],
+                    in1=s_sb[:, :, ns],
                     op0=ALU.mult,
                     op1=ALU.max,
                 )
                 nc.vector.scalar_tensor_tensor(
-                    out=weight[:, ns, :],
-                    in0=weight[:, ns, :],
+                    out=weight[:, :, ns],
+                    in0=weight[:, :, ns],
                     scalar=-2.0,
-                    in1=g_nj[:, ns, :],
+                    in1=g_sb[:, :, ns],
                     op0=ALU.mult,
                     op1=ALU.mult,
                 )
                 for n_cols in chunks:
                     nc.scalar.activation(
-                        out=denom[:, n_cols, :], in_=s_nj[:, n_cols, :], func=ACT.Square
+                        out=denom[:, :, n_cols], in_=s_sb[:, :, n_cols], func=ACT.Square
                     )
                 for n_cols in chunks:
                     nc.scalar.activation(
-                        out=denom[:, n_cols, :], in_=denom[:, n_cols, :], func=ACT.Square, bias=1.0
+                        out=denom[:, :, n_cols], in_=denom[:, :, n_cols], func=ACT.Square, bias=1.0
                     )
                 for n_cols in chunks:
                     nc.scalar.activation(
-                        out=recip[:, n_cols, :],
-                        in_=denom[:, n_cols, :],
+                        out=recip[:, :, n_cols],
+                        in_=denom[:, :, n_cols],
                         func=ACT.Abs_reciprocal_sqrt,
                     )
                 for n_cols in chunks:
                     nc.scalar.activation(
-                        out=recip[:, n_cols, :], in_=recip[:, n_cols, :], func=ACT.Square
+                        out=recip[:, :, n_cols], in_=recip[:, :, n_cols], func=ACT.Square
                     )
                 for n_cols in chunks:
                     nc.vector.scalar_tensor_tensor(
-                        out=check[:, n_cols, :],
-                        in0=denom[:, n_cols, :],
+                        out=check[:, :, n_cols],
+                        in0=denom[:, :, n_cols],
                         scalar=BIG,
-                        in1=recip[:, n_cols, :],
+                        in1=recip[:, :, n_cols],
                         op0=ALU.min,
                         op1=ALU.mult,
                     )
                 for n_cols in chunks:
                     nc.vector.scalar_tensor_tensor(
-                        out=check[:, n_cols, :],
-                        in0=check[:, n_cols, :],
+                        out=check[:, :, n_cols],
+                        in0=check[:, :, n_cols],
                         scalar=2.0,
-                        in1=recip[:, n_cols, :],
+                        in1=recip[:, :, n_cols],
                         op0=ALU.subtract,
                         op1=ALU.mult,
                     )
                 for n_cols in chunks:
-                    nc.vector.tensor_mul(
-                        out=ds_bf[:, n_cols, :], in0=weight[:, n_cols, :], in1=check[:, n_cols, :]
+                    nc.vector.tensor_tensor(
+                        out=ds_bf[:, n_cols, :].rearrange("p (m i) j -> p m j i", i=2),
+                        in0=weight[:, :, n_cols].rearrange("p j (m i) -> p m j i", i=2),
+                        in1=check[:, :, n_cols].rearrange("p j (m i) -> p m j i", i=2),
+                        op=ALU.mult,
                     )
                 nc.vector.quantize_mx(
                     out=ds_codes[:, ns].bitcast(E5M2_X4),
@@ -151,11 +152,14 @@ def tile_digitcaps_v_kernel(tc, x, W, s, grad_out, out):
                     )
                 x_codes = keep.tile([PARTS, TILE_COLS], U32, align_bytes=64, name="x_codes%d" % t)
                 x_scales = keep.tile([PARTS, TILE_COLS], U8, align_bytes=64, name="x_scales%d" % t)
-                nc.vector.quantize_mx(
-                    out=x_codes[:].bitcast(E4M3_X4),
-                    scales=x_scales[:],
-                    in_=grouped[:].rearrange("p e q j -> p (e q j)"),
-                )
+                for half in range(2):
+                    es = slice(half * E_HALF, (half + 1) * E_HALF)
+                    half_cols = slice(half * E_HALF * Q_TILE, (half + 1) * E_HALF * Q_TILE)
+                    nc.vector.quantize_mx(
+                        out=x_codes[:, half_cols].bitcast(E4M3_X4),
+                        scales=x_scales[:, half_cols],
+                        in_=grouped[:, es, :, :].rearrange("p e q j -> p (e q j)"),
+                    )
 
                 flat = flats.tile([PARTS, E, N], F32)
                 for e in range(E):

@@ -52,8 +52,10 @@ def tile_digitcaps_v_kernel(tc, x, W, s, grad_out, out):
             g_sb = head.tile([PARTS, PACK, N], BF16)
             for n_half in range(2):
                 ns = slice(n_half * N_HALF, (n_half + 1) * N_HALF)
-                nc.sync.dma_start(out=s_sb[:, :, ns], in_=s_rows[:, :, ns])
-            nc.sync.dma_start(out=g_sb[:], in_=g_rows)
+                for c in range(N_HALF // N_CHUNK):
+                    n_cols = slice(n_half * N_HALF + c * N_CHUNK, n_half * N_HALF + (c + 1) * N_CHUNK)
+                    nc.sync.dma_start(out=s_sb[:, :, n_cols], in_=s_rows[:, :, n_cols])
+                nc.sync.dma_start(out=g_sb[:, :, ns], in_=g_rows[:, :, ns])
             for t in range(TILES):
                 nc.sync.dma_start(
                     out=x_sb[t][:], in_=x_rows[:, :, t * TILE_COLS : (t + 1) * TILE_COLS]
@@ -70,22 +72,24 @@ def tile_digitcaps_v_kernel(tc, x, W, s, grad_out, out):
                     slice(n_half * N_HALF + c * N_CHUNK, n_half * N_HALF + (c + 1) * N_CHUNK)
                     for c in range(N_HALF // N_CHUNK)
                 ]
-                nc.vector.scalar_tensor_tensor(
-                    out=weight[:, :, ns],
-                    in0=s_sb[:, :, ns],
-                    scalar=-1.0,
-                    in1=s_sb[:, :, ns],
-                    op0=ALU.mult,
-                    op1=ALU.max,
-                )
-                nc.vector.scalar_tensor_tensor(
-                    out=weight[:, :, ns],
-                    in0=weight[:, :, ns],
-                    scalar=-2.0,
-                    in1=g_sb[:, :, ns],
-                    op0=ALU.mult,
-                    op1=ALU.mult,
-                )
+                for n_cols in chunks:
+                    nc.vector.scalar_tensor_tensor(
+                        out=weight[:, :, n_cols],
+                        in0=s_sb[:, :, n_cols],
+                        scalar=-1.0,
+                        in1=s_sb[:, :, n_cols],
+                        op0=ALU.mult,
+                        op1=ALU.max,
+                    )
+                for n_cols in chunks:
+                    nc.vector.scalar_tensor_tensor(
+                        out=weight[:, :, n_cols],
+                        in0=weight[:, :, n_cols],
+                        scalar=-2.0,
+                        in1=g_sb[:, :, n_cols],
+                        op0=ALU.mult,
+                        op1=ALU.mult,
+                    )
                 for n_cols in chunks:
                     nc.scalar.activation(
                         out=denom[:, :, n_cols], in_=s_sb[:, :, n_cols], func=ACT.Square
@@ -162,9 +166,29 @@ def tile_digitcaps_v_kernel(tc, x, W, s, grad_out, out):
                     )
 
                 flat = flats.tile([PARTS, E, N], F32)
+                stages = [stores.tile([PARTS, N_HALF, E], F32, name="stage") for h in range(2)]
+
+                def interleave(e_half, n_half):
+                    es = slice(e_half * E_HALF, (e_half + 1) * E_HALF)
+                    ns = slice(n_half * N_HALF, (n_half + 1) * N_HALF)
+                    nc.vector.tensor_copy(
+                        out=stages[n_half][:, :, es].rearrange("p (m i) e -> p m e i", i=2),
+                        in_=flat[:, es, ns].rearrange("p e (m i) -> p m e i", i=2),
+                    )
+
+                def store(n_half):
+                    nc.sync.dma_start(
+                        out=out_rows[
+                            t * Q_TILE : (t + 1) * Q_TILE, n_half * N_HALF * E : (n_half + 1) * N_HALF * E
+                        ],
+                        in_=stages[n_half][:].rearrange("p n e -> p (n e)"),
+                    )
+
+                banks = []
                 for e in range(E):
                     q_cols = slice(e * Q_TILE, (e + 1) * Q_TILE)
                     acc = psum.tile([PARTS, N], F32)
+                    banks.append(acc)
                     nc.tensor.matmul_mx(
                         out=acc[:],
                         lhsT=x_codes[:, q_cols].bitcast(E4M3_X4),
@@ -174,21 +198,24 @@ def tile_digitcaps_v_kernel(tc, x, W, s, grad_out, out):
                         start=True,
                         stop=True,
                     )
-                    nc.scalar.mul(out=flat[:, e, :], in_=acc[:], mul=1.0 / CAPS)
-
-                stages = [stores.tile([PARTS, N_HALF, E], F32, name="stage") for h in range(2)]
-                for e_half in range(2):
-                    es = slice(e_half * E_HALF, (e_half + 1) * E_HALF)
+                    if t < TILES - 1:
+                        nc.scalar.mul(out=flat[:, e, :], in_=acc[:], mul=1.0 / CAPS)
+                if t < TILES - 1:
+                    for e_half in range(2):
+                        for n_half in range(2):
+                            interleave(e_half, n_half)
+                    for n_half in range(2):
+                        store(n_half)
+                else:
                     for n_half in range(2):
                         ns = slice(n_half * N_HALF, (n_half + 1) * N_HALF)
-                        nc.vector.tensor_copy(
-                            out=stages[n_half][:, :, es].rearrange("p (m i) e -> p m e i", i=2),
-                            in_=flat[:, es, ns].rearrange("p e (m i) -> p m e i", i=2),
-                        )
-                for n_half in range(2):
-                    nc.sync.dma_start(
-                        out=out_rows[
-                            t * Q_TILE : (t + 1) * Q_TILE, n_half * N_HALF * E : (n_half + 1) * N_HALF * E
-                        ],
-                        in_=stages[n_half][:].rearrange("p n e -> p (n e)"),
-                    )
+                        for e in range(E):
+                            if e % E_HALF == E_HALF - 1:
+                                nc.vector.tensor_scalar_mul(
+                                    out=flat[:, e, ns], in0=banks[e][:, ns], scalar1=1.0 / CAPS
+                                )
+                            else:
+                                nc.scalar.mul(out=flat[:, e, ns], in_=banks[e][:, ns], mul=1.0 / CAPS)
+                        for e_half in range(2):
+                            interleave(e_half, n_half)
+                        store(n_half)

import concourse.mybir as mybir

F32 = mybir.dt.float32
BF16 = mybir.dt.bfloat16
U32 = mybir.dt.uint32
U8 = mybir.dt.uint8
E4M3_X4 = mybir.dt.float8_e4m3fn_x4
E5M2_X4 = mybir.dt.float8_e5m2_x4
ACT = mybir.ActivationFunctionType

PARTS = 128
PACK = 4
BATCH = PARTS * PACK
CAPS = 1152
E = 8
N = 512
Q_TILE = PARTS
TILES = CAPS // Q_TILE
TILE_COLS = Q_TILE * E
E_HALF = E // 2
N_CHUNK = 128
N_HALF = N // 2
BIG = 3.0e38
SCALAR_TILES = (1, 2)

FLOPS = 2 * BATCH * CAPS * E * N
BYTES = BATCH * CAPS * E * 2 + BATCH * N * 4 + BATCH * N * 2 + CAPS * E * N * 4
ALU = mybir.AluOpType


def tile_digitcaps_v_kernel(tc, x, W, s, grad_out, out):
    nc = tc.nc

    x_rows = x.rearrange("(p j) q e -> p j (q e)", j=PACK)
    s_rows = s.rearrange("(p j) c d -> p j (c d)", j=PACK)
    g_rows = grad_out.rearrange("(p j) c d o -> p j (c d o)", j=PACK)
    out_rows = out.rearrange("o q c d e -> (o q) (c d e)")

    with tc.tile_pool(name="keep", bufs=1) as keep, tc.tile_pool(name="work", bufs=3) as work:
        ds_codes = keep.tile([PARTS, N], U32, align_bytes=64)
        ds_scales = keep.tile([PARTS, N], U8, align_bytes=64)
        x_sb = [
            keep.tile([PARTS, PACK, TILE_COLS], BF16, name="x_tile%d" % t) for t in range(TILES)
        ]

        with tc.tile_pool(name="head", bufs=1) as head:
            warm = head.tile([PARTS, 2], F32)
            nc.vector.memset(warm[:, 0:1], 1.0)
            nc.scalar.activation(out=warm[:, 1:2], in_=warm[:, 0:1], func=ACT.Abs_reciprocal_sqrt)

            s_sb = head.tile([PARTS, PACK, N], F32)
            g_sb = head.tile([PARTS, PACK, N], BF16)
            for n_half in range(2):
                ns = slice(n_half * N_HALF, (n_half + 1) * N_HALF)
                for c in range(N_HALF // N_CHUNK):
                    n_cols = slice(n_half * N_HALF + c * N_CHUNK, n_half * N_HALF + (c + 1) * N_CHUNK)
                    nc.sync.dma_start(out=s_sb[:, :, n_cols], in_=s_rows[:, :, n_cols])
                nc.sync.dma_start(out=g_sb[:, :, ns], in_=g_rows[:, :, ns])
            for t in range(TILES):
                nc.sync.dma_start(
                    out=x_sb[t][:], in_=x_rows[:, :, t * TILE_COLS : (t + 1) * TILE_COLS]
                )

            weight = head.tile([PARTS, PACK, N], F32)
            denom = head.tile([PARTS, PACK, N], F32)
            recip = head.tile([PARTS, PACK, N], F32)
            check = head.tile([PARTS, PACK, N], F32)
            ds_bf = head.tile([PARTS, N, PACK], BF16, align_bytes=64)
            for n_half in range(2):
                ns = slice(n_half * N_HALF, (n_half + 1) * N_HALF)
                chunks = [
                    slice(n_half * N_HALF + c * N_CHUNK, n_half * N_HALF + (c + 1) * N_CHUNK)
                    for c in range(N_HALF // N_CHUNK)
                ]
                for n_cols in chunks:
                    nc.vector.scalar_tensor_tensor(
                        out=weight[:, :, n_cols],
                        in0=s_sb[:, :, n_cols],
                        scalar=-1.0,
                        in1=s_sb[:, :, n_cols],
                        op0=ALU.mult,
                        op1=ALU.max,
                    )
                for n_cols in chunks:
                    nc.vector.scalar_tensor_tensor(
                        out=weight[:, :, n_cols],
                        in0=weight[:, :, n_cols],
                        scalar=-2.0,
                        in1=g_sb[:, :, n_cols],
                        op0=ALU.mult,
                        op1=ALU.mult,
                    )
                for n_cols in chunks:
                    nc.scalar.activation(
                        out=denom[:, :, n_cols], in_=s_sb[:, :, n_cols], func=ACT.Square
                    )
                for n_cols in chunks:
                    nc.scalar.activation(
                        out=denom[:, :, n_cols], in_=denom[:, :, n_cols], func=ACT.Square, bias=1.0
                    )
                for n_cols in chunks:
                    nc.scalar.activation(
                        out=recip[:, :, n_cols],
                        in_=denom[:, :, n_cols],
                        func=ACT.Abs_reciprocal_sqrt,
                    )
                for n_cols in chunks:
                    nc.scalar.activation(
                        out=recip[:, :, n_cols], in_=recip[:, :, n_cols], func=ACT.Square
                    )
                for n_cols in chunks:
                    nc.vector.scalar_tensor_tensor(
                        out=check[:, :, n_cols],
                        in0=denom[:, :, n_cols],
                        scalar=BIG,
                        in1=recip[:, :, n_cols],
                        op0=ALU.min,
                        op1=ALU.mult,
                    )
                for n_cols in chunks:
                    nc.vector.scalar_tensor_tensor(
                        out=check[:, :, n_cols],
                        in0=check[:, :, n_cols],
                        scalar=2.0,
                        in1=recip[:, :, n_cols],
                        op0=ALU.subtract,
                        op1=ALU.mult,
                    )
                for n_cols in chunks:
                    nc.vector.tensor_tensor(
                        out=ds_bf[:, n_cols, :].rearrange("p (m i) j -> p m j i", i=2),
                        in0=weight[:, :, n_cols].rearrange("p j (m i) -> p m j i", i=2),
                        in1=check[:, :, n_cols].rearrange("p j (m i) -> p m j i", i=2),
                        op=ALU.mult,
                    )
                nc.vector.quantize_mx(
                    out=ds_codes[:, ns].bitcast(E5M2_X4),
                    scales=ds_scales[:, ns],
                    in_=ds_bf[:, ns, :].rearrange("p n j -> p (n j)"),
                )

        with (
            tc.tile_pool(name="flats", bufs=2) as flats,
            tc.tile_pool(name="stores", bufs=6) as stores,
            tc.psum_pool(name="psum", bufs=8) as psum,
        ):
            for t in range(TILES):
                x_qje = x_sb[t][:].rearrange("p j (q e) -> p q j e", e=E)
                grouped = work.tile([PARTS, E, Q_TILE, PACK], BF16, align_bytes=64)
                regroup = nc.scalar.copy if t in SCALAR_TILES else nc.vector.tensor_copy
                for half in range(2):
                    es = slice(half * E_HALF, (half + 1) * E_HALF)
                    regroup(
                        out=grouped[:, es, :, :].rearrange("p e q j -> p q j e"),
                        in_=x_qje[:, :, :, es],
                    )
                x_codes = keep.tile([PARTS, TILE_COLS], U32, align_bytes=64, name="x_codes%d" % t)
                x_scales = keep.tile([PARTS, TILE_COLS], U8, align_bytes=64, name="x_scales%d" % t)
                for half in range(2):
                    es = slice(half * E_HALF, (half + 1) * E_HALF)
                    half_cols = slice(half * E_HALF * Q_TILE, (half + 1) * E_HALF * Q_TILE)
                    nc.vector.quantize_mx(
                        out=x_codes[:, half_cols].bitcast(E4M3_X4),
                        scales=x_scales[:, half_cols],
                        in_=grouped[:, es, :, :].rearrange("p e q j -> p (e q j)"),
                    )

                flat = flats.tile([PARTS, E, N], F32)
                stages = [stores.tile([PARTS, N_HALF, E], F32, name="stage") for h in range(2)]

                def interleave(e_half, n_half):
                    es = slice(e_half * E_HALF, (e_half + 1) * E_HALF)
                    ns = slice(n_half * N_HALF, (n_half + 1) * N_HALF)
                    nc.vector.tensor_copy(
                        out=stages[n_half][:, :, es].rearrange("p (m i) e -> p m e i", i=2),
                        in_=flat[:, es, ns].rearrange("p e (m i) -> p m e i", i=2),
                    )

                def store(n_half):
                    nc.sync.dma_start(
                        out=out_rows[
                            t * Q_TILE : (t + 1) * Q_TILE, n_half * N_HALF * E : (n_half + 1) * N_HALF * E
                        ],
                        in_=stages[n_half][:].rearrange("p n e -> p (n e)"),
                    )

                banks = []
                for e in range(E):
                    q_cols = slice(e * Q_TILE, (e + 1) * Q_TILE)
                    acc = psum.tile([PARTS, N], F32)
                    banks.append(acc)
                    nc.tensor.matmul_mx(
                        out=acc[:],
                        lhsT=x_codes[:, q_cols].bitcast(E4M3_X4),
                        lhsT_scale=x_scales[:, q_cols],
                        rhs=ds_codes[:].bitcast(E5M2_X4),
                        rhs_scale=ds_scales[:],
                        start=True,
                        stop=True,
                    )
                    if t < TILES - 1:
                        nc.scalar.mul(out=flat[:, e, :], in_=acc[:], mul=1.0 / CAPS)
                if t < TILES - 1:
                    for e_half in range(2):
                        for n_half in range(2):
                            interleave(e_half, n_half)
                    for n_half in range(2):
                        store(n_half)
                else:
                    for n_half in range(2):
                        ns = slice(n_half * N_HALF, (n_half + 1) * N_HALF)
                        for e in range(E):
                            if e % E_HALF == E_HALF - 1:
                                nc.vector.tensor_scalar_mul(
                                    out=flat[:, e, ns], in0=banks[e][:, ns], scalar1=1.0 / CAPS
                                )
                            else:
                                nc.scalar.mul(out=flat[:, e, ns], in_=banks[e][:, ns], mul=1.0 / CAPS)
                        for e_half in range(2):
                            interleave(e_half, n_half)
                        store(n_half)
